import numpy as np
import ml_dtypes


def mxq(x, axis, fmt="e4m3"):
    dtype, down = {"e4m3": (ml_dtypes.float8_e4m3fn, 7), "e5m2": (ml_dtypes.float8_e5m2, 14)}[fmt]
    v = np.moveaxis(np.asarray(x, np.float32).astype(ml_dtypes.bfloat16).astype(np.float64), axis, -1)
    blocks = v.reshape(v.shape[:-1] + (-1, 32))
    amax = np.abs(blocks).max(-1, keepdims=True)
    byte = np.maximum(np.where(amax > 0, np.frexp(amax)[1] - 1 + 127, 0) - down, 1)
    scale = np.exp2(byte - 127.0)
    codes = (blocks / scale).astype(np.float32).astype(dtype).astype(np.float64)
    return np.moveaxis((codes * scale).reshape(v.shape), -1, axis)


WIDE = False


def mx_kscale(k):
    if not WIDE:
        return np.ones(k)
    levels = np.array([10, -10, 5, -5, 0])
    a = np.random.permutation(np.resize(levels, k // 512 * 4)).reshape(k // 512, 4)
    idx = np.arange(k)
    return np.exp2(a[idx // 512, idx % 128 // 32])


BF16 = ml_dtypes.bfloat16


def bf(x):
    return np.asarray(x, np.float32).astype(BF16)


def f64(x):
    return np.asarray(x).astype(np.float64)


E2M1 = np.array([0.0, 0.5, 1.0, 1.5, 2.0, 3.0, 4.0, 6.0, -0.0, -0.5, -1.0, -1.5, -2.0, -3.0, -4.0, -6.0])


def pack_weight(w, fmt):
    k, n = w.shape
    w = f64(bf(w)).reshape(k // 32, 32, n)
    amax = np.abs(w).max(1)
    if fmt == "e4m3":
        byte = np.frexp(amax)[1] - 1 + 127 - 7
    else:
        mant, ex = np.frexp(amax / 6.0)
        byte = np.where(mant > 0.5, ex, ex - 1) + 127
    byte = np.clip(np.where(amax > 0, byte, 1), 1, 254)
    scaled = (w * np.exp2(127.0 - byte)[:, None, :]).reshape(k, n).astype(np.float32)
    by_word = np.ascontiguousarray(scaled.reshape(k // 512, 128, 4, n).transpose(0, 1, 3, 2))
    if fmt == "e4m3":
        words = by_word.astype(ml_dtypes.float8_e4m3fn).view(np.uint8)
    else:
        c = by_word.astype(ml_dtypes.float4_e2m1fn).view(np.uint8) & 0xF
        words = c[..., 0::2] | (c[..., 1::2] << 4)
    return np.ascontiguousarray(words), np.ascontiguousarray(byte.astype(np.uint8).reshape(k // 512, 16, n))


def unpack_weight(words, scales, fmt):
    g, p, n, _ = words.shape
    if fmt == "e4m3":
        vals = np.ascontiguousarray(words).view(ml_dtypes.float8_e4m3fn).astype(np.float64)
    else:
        nib = np.empty((g, p, n, 4), np.uint8)
        nib[..., 0::2] = words & 0xF
        nib[..., 1::2] = words >> 4
        vals = E2M1[nib]
    vals = vals * np.repeat(np.exp2(scales.astype(np.float64) - 127.0), 8, axis=1)[..., None]
    return vals.transpose(0, 1, 3, 2).reshape(g * 512, n)


B, S, H = 2, 512, 1024
GAMMA = 0.96875


def sigmoid(v):
    return 1.0 / (1.0 + np.exp(-v))


def setup_inputs():
    s, u = mx_kscale(H), mx_kscale(H)
    a = 1.4 / H ** 0.25
    q = bf(np.random.standard_normal((B, S, H)) * a * s)
    k = bf(np.random.standard_normal((B, S, H)) * a / s)
    x = bf(np.random.standard_normal((B, S, H)) * u)
    words, scales = pack_weight(np.random.standard_normal((H, H)) * 0.5 / np.sqrt(H) / u[:, None], "e4m3")
    return {"q": q, "k": k, "x": x, "w_v_words": words, "w_v_scales": scales}


def reference(q, k, x, w_v_words, w_v_scales):
    idx = f64(np.arange(S))
    decay = GAMMA ** np.abs(idx[None, :] - idx[:, None])
    scores = (mxq(f64(q), 2, "e4m3") @ mxq(f64(k), 2, "e4m3").transpose(0, 2, 1)) * decay
    g = scores * sigmoid(scores)
    v = mxq(f64(x), 2, "e4m3") @ unpack_weight(w_v_words, w_v_scales, "e4m3")
    return mxq(g, 2, "e4m3") @ mxq(v, 1, "e4m3")

@@ -1,0 +1,241 @@
+import math
+from contextlib import ExitStack
+
+import concourse.mybir as mybir
+from concourse.masks import make_identity
+
+F32 = mybir.dt.float32
+BF16 = mybir.dt.bfloat16
+I32 = mybir.dt.int32
+U32 = mybir.dt.uint32
+U8 = mybir.dt.uint8
+FP8X4 = mybir.dt.float8_e4m3fn_x4
+ACT = mybir.ActivationFunctionType
+ALU = mybir.AluOpType
+
+B = 2
+S = 512
+H = 1024
+GAMMA = 0.96875
+P = 128
+PACK = 4
+K_PASS = P * PACK
+PASSES = H // K_PASS
+TILES = S // P
+WORDS = K_PASS // 2
+BANK = 512
+BANKS = 8
+HALVES = H // BANK
+KEYS = "(p i) h -> i p h"
+QUERIES = "(i p) h -> i p h"
+
+FLOPS = 2 * B * (S * H * H + 2 * S * S * H)
+
+
+def tile_simpleretention_pa_kernel(tc, q, k, x, w_v_words, w_v_scales, out):
+    nc = tc.nc
+    with ExitStack() as ctx:
+        keep = ctx.enter_context(tc.tile_pool(name="keep", bufs=1))
+        stage = ctx.enter_context(tc.tile_pool(name="stage", bufs=4))
+        results = ctx.enter_context(tc.tile_pool(name="results", bufs=S * H // (P * BANK)))
+        psum = ctx.enter_context(tc.psum_pool(name="psum", bufs=BANKS))
+        ctx.enter_context(tc.manual_schedule())
+
+        w_scales = keep.tile([P, PASSES, H], U8, align_bytes=64)
+        nc.vector.memset(w_scales[:].bitcast(I32), 0)
+        ident = keep.tile([P, P], F32)
+        make_identity(nc, ident[:])
+        offset = keep.tile([P, S + PACK - 1], F32)
+        nc.gpsimd.iota(
+            offset[:],
+            pattern=[[1, S + PACK - 1]],
+            base=-(PACK - 1),
+            channel_multiplier=-PACK,
+            allow_small_or_imprecise_dtypes=True,
+        )
+        distance = keep.tile([P, S + PACK - 1], F32)
+        nc.vector.scalar_tensor_tensor(
+            out=distance[:], in0=offset[:], scalar=-1.0, in1=offset[:], op0=ALU.mult, op1=ALU.max
+        )
+        first_exp = keep.tile([P, 1], F32)
+        nc.scalar.activation(out=first_exp[:], in_=ident[:, 0:1], func=ACT.Exp)
+
+        def load_tokens(rows, view, name):
+            raw = keep.tile([P, TILES, H], BF16, name=name)
+            tiles = rows.rearrange(view, p=P)
+            for i in range(TILES):
+                nc.sync.dma_start(out=raw[:, i, :], in_=tiles[i])
+            return raw
+
+        x_raw0 = load_tokens(x[0], KEYS, "x_raw0")
+        for quadrant in range(4):
+            nc.sync.dma_start(
+                out=w_scales[32 * quadrant : 32 * quadrant + 4].bitcast(I32),
+                in_=w_v_scales[:, 4 * quadrant : 4 * quadrant + 4, :]
+                .rearrange("c r j -> r c j")
+                .bitcast(I32),
+            )
+        w_words = keep.tile([P, PASSES, H], U32, align_bytes=64)
+        w_bytes = w_v_words.rearrange("c p j t -> p c (j t)")
+        for half in range(HALVES):
+            nc.sync.dma_start(
+                out=w_words[:, :, half * BANK : (half + 1) * BANK].bitcast(I32),
+                in_=w_bytes[:, :, half * BANK * PACK : (half + 1) * BANK * PACK].bitcast(I32),
+            )
+        k_raw0 = load_tokens(k[0], KEYS, "k_raw0")
+        q_raw0 = load_tokens(q[0], QUERIES, "q_raw0")
+        x_raw1 = load_tokens(x[1], KEYS, "x_raw1")
+        k_raw1 = load_tokens(k[1], KEYS, "k_raw1")
+        q_raw1 = load_tokens(q[1], QUERIES, "q_raw1")
+
+        def mx_operand(name, shape):
+            codes = keep.tile(shape, U32, name=name + "_codes", align_bytes=64)
+            scales = keep.tile(shape, U8, name=name + "_scales", align_bytes=64)
+            return codes, scales
+
+        def quantise(grouped, codes, scales):
+            nc.vector.quantize_mx(out=codes.bitcast(FP8X4), scales=scales, in_=grouped)
+
+        def regroup(index, grouped, bank_view):
+            if index % 4 == 1:
+                nc.vector.tensor_copy(out=grouped, in_=bank_view)
+            else:
+                nc.scalar.copy(out=grouped, in_=bank_view)
+
+        def quantise_features(raw, every_second_word, name):
+            codes, scales = mx_operand(name, [P, TILES, PASSES, P])
+            words = raw[:].bitcast(F32)
+            waiting = []
+            for i in range(TILES):
+                bank = psum.tile([P, PASSES, 2, P], F32, tag="bank")
+                for c in range(PASSES):
+                    for u in range(2):
+                        if every_second_word:
+                            cols = slice(WORDS * c + u, WORDS * (c + 1), 2)
+                        else:
+                            cols = slice(WORDS * c + P * u, WORDS * c + P * (u + 1))
+                        nc.tensor.transpose(bank[:, c, u, :], words[:, i, cols], ident[:])
+                grouped = stage.tile([P, PASSES, P, PACK], BF16, align_bytes=64)
+                regroup(i, grouped[:].bitcast(F32), bank[:].rearrange("p c u r -> p c r u"))
+                waiting.append(
+                    (
+                        grouped[:].rearrange("p c r t -> p (c r t)"),
+                        codes[:, i].rearrange("p c r -> p (c r)"),
+                        scales[:, i].rearrange("p c r -> p (c r)"),
+                    )
+                )
+                if i > 0:
+                    quantise(*waiting[i - 1])
+            quantise(*waiting[TILES - 1])
+            return codes, scales
+
+        def build_decay():
+            decay = keep.tile([P, PACK, S], F32)
+            for i in range(PACK):
+                first = PACK - 1 - i
+                nc.scalar.activation(
+                    out=decay[:, i, :],
+                    in_=distance[:, first : first + S],
+                    func=ACT.Exp,
+                    scale=math.log(GAMMA),
+                )
+            return decay
+
+        def project_values(x_codes, x_scales, v_codes, v_scales, half):
+            waiting = []
+            for n in range(BANK // P):
+                cols = slice(half * BANK + n * P, half * BANK + (n + 1) * P)
+                bank = psum.tile([P, TILES, P], F32, tag="bank")
+                for i in range(TILES):
+                    for c in range(PASSES):
+                        nc.tensor.matmul_mx(
+                            out=bank[:, i, :],
+                            lhsT=x_codes[:, i, c, :].bitcast(FP8X4),
+                            lhsT_scale=x_scales[:, i, c, :],
+                            rhs=w_words[:, c, cols].bitcast(FP8X4),
+                            rhs_scale=w_scales[:, c, cols],
+                            start=(c == 0),
+                            stop=(c == PASSES - 1),
+                        )
+                v_grouped = stage.tile([P, P, PACK], BF16, align_bytes=64)
+                regroup(n, v_grouped[:], bank[:].rearrange("p i j -> p j i"))
+                waiting.append(
+                    (v_grouped[:].rearrange("p j i -> p (j i)"), v_codes[:, cols], v_scales[:, cols])
+                )
+                if n > 0:
+                    quantise(*waiting[n - 1])
+            quantise(*waiting[BANK // P - 1])
+
+        def gate_scores(q_codes, q_scales, k_codes, k_scales, decay, name):
+            g_codes, g_scales = mx_operand(name, [P, S])
+            waiting = []
+            for mc in range(TILES):
+                cols = slice(mc * P, (mc + 1) * P)
+                bank = psum.tile([P, TILES, P], F32, tag="bank")
+                for i in range(TILES):
+                    for c in range(PASSES):
+                        nc.tensor.matmul_mx(
+                            out=bank[:, i, :],
+                            lhsT=k_codes[:, i, c, :].bitcast(FP8X4),
+                            lhsT_scale=k_scales[:, i, c, :],
+                            rhs=q_codes[:, mc, c, :].bitcast(FP8X4),
+                            rhs_scale=q_scales[:, mc, c, :],
+                            start=(c == 0),
+                            stop=(c == PASSES - 1),
+                        )
+                decayed = stage.tile([P, P, PACK], F32)
+                nc.vector.tensor_tensor(
+                    out=decayed[:],
+                    in0=bank[:].rearrange("p i m -> p m i"),
+                    in1=decay[:, :, cols].rearrange("p i m -> p m i"),
+                    op=ALU.mult,
+                )
+                g_grouped = stage.tile([P, P, PACK], BF16, align_bytes=64)
+                nc.scalar.activation(out=g_grouped[:], in_=decayed[:], func=ACT.Silu)
+                waiting.append(
+                    (g_grouped[:].rearrange("p m i -> p (m i)"), g_codes[:, cols], g_scales[:, cols])
+                )
+                if mc > 0:
+                    quantise(*waiting[mc - 1])
+            quantise(*waiting[TILES - 1])
+            return g_codes, g_scales
+
+        def write_outputs(b, g_codes, g_scales, v_codes, v_scales):
+            for half in range(HALVES):
+                cols = slice(half * BANK, (half + 1) * BANK)
+                for mc in range(TILES):
+                    rows = slice(mc * P, (mc + 1) * P)
+                    bank = psum.tile([P, BANK], F32, tag="bank")
+                    nc.tensor.matmul_mx(
+                        out=bank[:],
+                        lhsT=g_codes[:, rows].bitcast(FP8X4),
+                        lhsT_scale=g_scales[:, rows],
+                        rhs=v_codes[:, cols].bitcast(FP8X4),
+                        rhs_scale=v_scales[:, cols],
+                        start=True,
+                        stop=True,
+                    )
+                    piece = results.tile([P, BANK], F32)
+                    if mc % 2 == 0:
+                        nc.scalar.copy(out=piece[:], in_=bank[:])
+                    else:
+                        nc.vector.tensor_copy(out=piece[:], in_=bank[:])
+                    nc.sync.dma_start(out=out[b, rows, cols], in_=piece[:])
+
+        v_mx0 = mx_operand("v0", [P, H])
+        v_mx1 = mx_operand("v1", [P, H])
+        x_mx0 = quantise_features(x_raw0, True, "x0")
+        decay = build_decay()
+        project_values(*x_mx0, *v_mx0, 0)
+        project_values(*x_mx0, *v_mx0, 1)
+        k_mx0 = quantise_features(k_raw0, False, "k0")
+        q_mx0 = quantise_features(q_raw0, False, "q0")
+        g_mx0 = gate_scores(*q_mx0, *k_mx0, decay, "g0")
+        x_mx1 = quantise_features(x_raw1, True, "x1")
+        write_outputs(0, *g_mx0, *v_mx0)
+        project_values(*x_mx1, *v_mx1, 0)
+        k_mx1 = quantise_features(k_raw1, False, "k1")
+        q_mx1 = quantise_features(q_raw1, False, "q1")
+        g_mx1 = gate_scores(*q_mx1, *k_mx1, decay, "g1")
+        project_values(*x_mx1, *v_mx1, 1)
+        write_outputs(1, *g_mx1, *v_mx1)

@@ -36,7 +36,7 @@ def tile_simpleretention_pa_kernel(tc, q, k, x, w_v_words, w_v_scales, out):
     nc = tc.nc
     with ExitStack() as ctx:
         keep = ctx.enter_context(tc.tile_pool(name="keep", bufs=1))
-        stage = ctx.enter_context(tc.tile_pool(name="stage", bufs=4))
+        stage = ctx.enter_context(tc.tile_pool(name="stage", bufs=6))
         results = ctx.enter_context(tc.tile_pool(name="results", bufs=S * H // (P * BANK)))
         psum = ctx.enter_context(tc.psum_pool(name="psum", bufs=BANKS))
         ctx.enter_context(tc.manual_schedule())
@@ -67,7 +67,9 @@ def tile_simpleretention_pa_kernel(tc, q, k, x, w_v_words, w_v_scales, out):
                 nc.sync.dma_start(out=raw[:, i, :], in_=tiles[i])
             return raw
 
-        x_raw0 = load_tokens(x[0], KEYS, "x_raw0")
+        x_raw = [load_tokens(x[0], KEYS, "x_raw0")]
+        k_raw = []
+        q_raw = []
         for quadrant in range(4):
             nc.sync.dma_start(
                 out=w_scales[32 * quadrant : 32 * quadrant + 4].bitcast(I32),
@@ -82,11 +84,11 @@ def tile_simpleretention_pa_kernel(tc, q, k, x, w_v_words, w_v_scales, out):
                 out=w_words[:, :, half * BANK : (half + 1) * BANK].bitcast(I32),
                 in_=w_bytes[:, :, half * BANK * PACK : (half + 1) * BANK * PACK].bitcast(I32),
             )
-        k_raw0 = load_tokens(k[0], KEYS, "k_raw0")
-        q_raw0 = load_tokens(q[0], QUERIES, "q_raw0")
-        x_raw1 = load_tokens(x[1], KEYS, "x_raw1")
-        k_raw1 = load_tokens(k[1], KEYS, "k_raw1")
-        q_raw1 = load_tokens(q[1], QUERIES, "q_raw1")
+        for b in range(B):
+            k_raw.append(load_tokens(k[b], KEYS, "k_raw%d" % b))
+            q_raw.append(load_tokens(q[b], QUERIES, "q_raw%d" % b))
+            if b + 1 < B:
+                x_raw.append(load_tokens(x[b + 1], KEYS, "x_raw%d" % (b + 1)))
 
         def mx_operand(name, shape):
             codes = keep.tile(shape, U32, name=name + "_codes", align_bytes=64)
@@ -96,11 +98,11 @@ def tile_simpleretention_pa_kernel(tc, q, k, x, w_v_words, w_v_scales, out):
         def quantise(grouped, codes, scales):
             nc.vector.quantize_mx(out=codes.bitcast(FP8X4), scales=scales, in_=grouped)
 
-        def regroup(index, grouped, bank_view):
-            if index % 4 == 1:
-                nc.vector.tensor_copy(out=grouped, in_=bank_view)
+        def empty_bank(on_vector, out_view, bank_view):
+            if on_vector:
+                nc.vector.tensor_copy(out=out_view, in_=bank_view)
             else:
-                nc.scalar.copy(out=grouped, in_=bank_view)
+                nc.scalar.copy(out=out_view, in_=bank_view)
 
         def quantise_features(raw, every_second_word, name):
             codes, scales = mx_operand(name, [P, TILES, PASSES, P])
@@ -116,7 +118,9 @@ def tile_simpleretention_pa_kernel(tc, q, k, x, w_v_words, w_v_scales, out):
                             cols = slice(WORDS * c + P * u, WORDS * c + P * (u + 1))
                         nc.tensor.transpose(bank[:, c, u, :], words[:, i, cols], ident[:])
                 grouped = stage.tile([P, PASSES, P, PACK], BF16, align_bytes=64)
-                regroup(i, grouped[:].bitcast(F32), bank[:].rearrange("p c u r -> p c r u"))
+                empty_bank(
+                    i % 4 == 1, grouped[:].bitcast(F32), bank[:].rearrange("p c u r -> p c r u")
+                )
                 waiting.append(
                     (
                         grouped[:].rearrange("p c r t -> p (c r t)"),
@@ -141,10 +145,10 @@ def tile_simpleretention_pa_kernel(tc, q, k, x, w_v_words, w_v_scales, out):
                 )
             return decay
 
-        def project_values(x_codes, x_scales, v_codes, v_scales, half):
+        def project_values(x_codes, x_scales, v_codes, v_scales, blocks):
             waiting = []
-            for n in range(BANK // P):
-                cols = slice(half * BANK + n * P, half * BANK + (n + 1) * P)
+            for n in blocks:
+                cols = slice(n * P, (n + 1) * P)
                 bank = psum.tile([P, TILES, P], F32, tag="bank")
                 for i in range(TILES):
                     for c in range(PASSES):
@@ -158,13 +162,13 @@ def tile_simpleretention_pa_kernel(tc, q, k, x, w_v_words, w_v_scales, out):
                             stop=(c == PASSES - 1),
                         )
                 v_grouped = stage.tile([P, P, PACK], BF16, align_bytes=64)
-                regroup(n, v_grouped[:], bank[:].rearrange("p i j -> p j i"))
+                empty_bank(n % 2 == 1, v_grouped[:], bank[:].rearrange("p i j -> p j i"))
                 waiting.append(
                     (v_grouped[:].rearrange("p j i -> p (j i)"), v_codes[:, cols], v_scales[:, cols])
                 )
-                if n > 0:
-                    quantise(*waiting[n - 1])
-            quantise(*waiting[BANK // P - 1])
+                if len(waiting) > 1:
+                    quantise(*waiting[-2])
+            quantise(*waiting[-1])
 
         def gate_scores(q_codes, q_scales, k_codes, k_scales, decay, name):
             g_codes, g_scales = mx_operand(name, [P, S])
@@ -216,26 +220,19 @@ def tile_simpleretention_pa_kernel(tc, q, k, x, w_v_words, w_v_scales, out):
                         stop=True,
                     )
                     piece = results.tile([P, BANK], F32)
-                    if mc % 2 == 0:
-                        nc.scalar.copy(out=piece[:], in_=bank[:])
-                    else:
-                        nc.vector.tensor_copy(out=piece[:], in_=bank[:])
+                    empty_bank(mc % 2 == 1, piece[:], bank[:])
                     nc.sync.dma_start(out=out[b, rows, cols], in_=piece[:])
 
-        v_mx0 = mx_operand("v0", [P, H])
-        v_mx1 = mx_operand("v1", [P, H])
-        x_mx0 = quantise_features(x_raw0, True, "x0")
+        x_mx = quantise_features(x_raw[0], True, "x0")
         decay = build_decay()
-        project_values(*x_mx0, *v_mx0, 0)
-        project_values(*x_mx0, *v_mx0, 1)
-        k_mx0 = quantise_features(k_raw0, False, "k0")
-        q_mx0 = quantise_features(q_raw0, False, "q0")
-        g_mx0 = gate_scores(*q_mx0, *k_mx0, decay, "g0")
-        x_mx1 = quantise_features(x_raw1, True, "x1")
-        write_outputs(0, *g_mx0, *v_mx0)
-        project_values(*x_mx1, *v_mx1, 0)
-        k_mx1 = quantise_features(k_raw1, False, "k1")
-        q_mx1 = quantise_features(q_raw1, False, "q1")
-        g_mx1 = gate_scores(*q_mx1, *k_mx1, decay, "g1")
-        project_values(*x_mx1, *v_mx1, 1)
-        write_outputs(1, *g_mx1, *v_mx1)
+        for b in range(B):
+            v_mx = mx_operand("v%d" % b, [P, H])
+            project_values(*x_mx, *v_mx, range(0, 4))
+            k_mx = quantise_features(k_raw[b], False, "k%d" % b)
+            project_values(*x_mx, *v_mx, range(4, 6))
+            q_mx = quantise_features(q_raw[b], False, "q%d" % b)
+            project_values(*x_mx, *v_mx, range(6, 8))
+            g_mx = gate_scores(*q_mx, *k_mx, decay, "g%d" % b)
+            if b + 1 < B:
+                x_mx = quantise_features(x_raw[b + 1], True, "x%d" % (b + 1))
+            write_outputs(b, *g_mx, *v_mx)

@@ -53,12 +53,9 @@ def tile_simpleretention_pa_kernel(tc, q, k, x, w_v_words, w_v_scales, out):
             channel_multiplier=-PACK,
             allow_small_or_imprecise_dtypes=True,
         )
-        distance = keep.tile([P, S + PACK - 1], F32)
-        nc.vector.scalar_tensor_tensor(
-            out=distance[:], in0=offset[:], scalar=-1.0, in1=offset[:], op0=ALU.mult, op1=ALU.max
-        )
-        first_exp = keep.tile([P, 1], F32)
-        nc.scalar.activation(out=first_exp[:], in_=ident[:, 0:1], func=ACT.Exp)
+        falloff = keep.tile([P, S + PACK - 1], F32)
+        nc.scalar.activation(out=falloff[:], in_=offset[:], func=ACT.Abs)
+        nc.scalar.activation(out=falloff[:], in_=falloff[:], func=ACT.Exp, scale=math.log(GAMMA))
 
         def load_tokens(rows, view, name):
             raw = keep.tile([P, TILES, H], BF16, name=name)
@@ -137,12 +134,9 @@ def tile_simpleretention_pa_kernel(tc, q, k, x, w_v_words, w_v_scales, out):
             decay = keep.tile([P, PACK, S], F32)
             for i in range(PACK):
                 first = PACK - 1 - i
-                nc.scalar.activation(
-                    out=decay[:, i, :],
-                    in_=distance[:, first : first + S],
-                    func=ACT.Exp,
-                    scale=math.log(GAMMA),
-                )
+                nc.vector.tensor_copy(out=decay[:, i, :], in_=falloff[:, first : first + S])
+            first_silu = keep.tile([P, 1], F32)
+            nc.scalar.activation(out=first_silu[:], in_=falloff[:, 0:1], func=ACT.Silu)
             return decay
 
         def project_values(x_codes, x_scales, v_codes, v_scales, blocks):
@@ -162,7 +156,7 @@ def tile_simpleretention_pa_kernel(tc, q, k, x, w_v_words, w_v_scales, out):
                             stop=(c == PASSES - 1),
                         )
                 v_grouped = stage.tile([P, P, PACK], BF16, align_bytes=64)
-                empty_bank(n % 2 == 1, v_grouped[:], bank[:].rearrange("p i j -> p j i"))
+                empty_bank(n % 4 == 1, v_grouped[:], bank[:].rearrange("p i j -> p j i"))
                 waiting.append(
                     (v_grouped[:].rearrange("p j i -> p (j i)"), v_codes[:, cols], v_scales[:, cols])
                 )
@@ -205,10 +199,10 @@ def tile_simpleretention_pa_kernel(tc, q, k, x, w_v_words, w_v_scales, out):
             return g_codes, g_scales
 
         def write_outputs(b, g_codes, g_scales, v_codes, v_scales):
-            for half in range(HALVES):
-                cols = slice(half * BANK, (half + 1) * BANK)
-                for mc in range(TILES):
-                    rows = slice(mc * P, (mc + 1) * P)
+            for mc in range(TILES):
+                rows = slice(mc * P, (mc + 1) * P)
+                for half in range(HALVES):
+                    cols = slice(half * BANK, (half + 1) * BANK)
                     bank = psum.tile([P, BANK], F32, tag="bank")
                     nc.tensor.matmul_mx(
                         out=bank[:],
@@ -220,7 +214,7 @@ def tile_simpleretention_pa_kernel(tc, q, k, x, w_v_words, w_v_scales, out):
                         stop=True,
                     )
                     piece = results.tile([P, BANK], F32)
-                    empty_bank(mc % 2 == 1, piece[:], bank[:])
+                    empty_bank(half % 2 == 1, piece[:], bank[:])
                     nc.sync.dma_start(out=out[b, rows, cols], in_=piece[:])
 
         x_mx = quantise_features(x_raw[0], True, "x0")

@@ -131,10 +131,12 @@ def tile_simpleretention_pa_kernel(tc, q, k, x, w_v_words, w_v_scales, out):
             return codes, scales
 
         def build_decay():
-            decay = keep.tile([P, PACK, S], F32)
+            windows = keep.tile([P, PACK, S], F32)
             for i in range(PACK):
                 first = PACK - 1 - i
-                nc.vector.tensor_copy(out=decay[:, i, :], in_=falloff[:, first : first + S])
+                nc.vector.tensor_copy(out=windows[:, i, :], in_=falloff[:, first : first + S])
+            decay = keep.tile([P, S, PACK], F32)
+            nc.vector.tensor_copy(out=decay[:], in_=windows[:].rearrange("p i m -> p m i"))
             first_silu = keep.tile([P, 1], F32)
             nc.scalar.activation(out=first_silu[:], in_=falloff[:, 0:1], func=ACT.Silu)
             return decay
@@ -185,7 +187,7 @@ def tile_simpleretention_pa_kernel(tc, q, k, x, w_v_words, w_v_scales, out):
                 nc.vector.tensor_tensor(
                     out=decayed[:],
                     in0=bank[:].rearrange("p i m -> p m i"),
-                    in1=decay[:, :, cols].rearrange("p i m -> p m i"),
+                    in1=decay[:, cols, :],
                     op=ALU.mult,
                 )
                 g_grouped = stage.tile([P, P, PACK], BF16, align_bytes=64)

@@ -87,13 +87,21 @@ def tile_simpleretention_pa_kernel(tc, q, k, x, w_v_words, w_v_scales, out):
             if b + 1 < B:
                 x_raw.append(load_tokens(x[b + 1], KEYS, "x_raw%d" % (b + 1)))
 
+        held_back = []
+
+        def issue_held_back():
+            for grouped, codes, scales in held_back:
+                nc.vector.quantize_mx(out=codes.bitcast(FP8X4), scales=scales, in_=grouped)
+            held_back.clear()
+
+        def hold_back(grouped, codes, scales):
+            issue_held_back()
+            held_back.append((grouped, codes, scales))
+
         def mx_operand(name, shape):
             codes = keep.tile(shape, U32, name=name + "_codes", align_bytes=64)
             scales = keep.tile(shape, U8, name=name + "_scales", align_bytes=64)
             return codes, scales
-
-        def quantise(grouped, codes, scales):
-            nc.vector.quantize_mx(out=codes.bitcast(FP8X4), scales=scales, in_=grouped)
 
         def empty_bank(on_vector, out_view, bank_view):
             if on_vector:
@@ -101,134 +109,169 @@ def tile_simpleretention_pa_kernel(tc, q, k, x, w_v_words, w_v_scales, out):
             else:
                 nc.scalar.copy(out=out_view, in_=bank_view)
 
-        def quantise_features(raw, every_second_word, name):
-            codes, scales = mx_operand(name, [P, TILES, PASSES, P])
+        def transpose_tile(raw, every_second_word, operand, i):
+            codes, scales = operand
             words = raw[:].bitcast(F32)
-            waiting = []
+            bank = psum.tile([P, PASSES, 2, P], F32, tag="bank")
+            for c in range(PASSES):
+                for u in range(2):
+                    if every_second_word:
+                        cols = slice(WORDS * c + u, WORDS * (c + 1), 2)
+                    else:
+                        cols = slice(WORDS * c + P * u, WORDS * c + P * (u + 1))
+                    nc.tensor.transpose(bank[:, c, u, :], words[:, i, cols], ident[:])
+            grouped = stage.tile([P, PASSES, P, PACK], BF16, align_bytes=64)
+            empty_bank(
+                i % 4 == 1, grouped[:].bitcast(F32), bank[:].rearrange("p c u r -> p c r u")
+            )
+            hold_back(
+                grouped[:].rearrange("p c r t -> p (c r t)"),
+                codes[:, i].rearrange("p c r -> p (c r)"),
+                scales[:, i].rearrange("p c r -> p (c r)"),
+            )
+
+        def project_block(x_mx, v_mx, n):
+            x_codes, x_scales = x_mx
+            v_codes, v_scales = v_mx
+            cols = slice(n * P, (n + 1) * P)
+            bank = psum.tile([P, TILES, P], F32, tag="bank")
             for i in range(TILES):
-                bank = psum.tile([P, PASSES, 2, P], F32, tag="bank")
                 for c in range(PASSES):
-                    for u in range(2):
-                        if every_second_word:
-                            cols = slice(WORDS * c + u, WORDS * (c + 1), 2)
-                        else:
-                            cols = slice(WORDS * c + P * u, WORDS * c + P * (u + 1))
-                        nc.tensor.transpose(bank[:, c, u, :], words[:, i, cols], ident[:])
-                grouped = stage.tile([P, PASSES, P, PACK], BF16, align_bytes=64)
-                empty_bank(
-                    i % 4 == 1, grouped[:].bitcast(F32), bank[:].rearrange("p c u r -> p c r u")
-                )
-                waiting.append(
-                    (
-                        grouped[:].rearrange("p c r t -> p (c r t)"),
-                        codes[:, i].rearrange("p c r -> p (c r)"),
-                        scales[:, i].rearrange("p c r -> p (c r)"),
-                    )
-                )
-                if i > 0:
-                    quantise(*waiting[i - 1])
-            quantise(*waiting[TILES - 1])
-            return codes, scales
-
-        def build_decay():
-            windows = keep.tile([P, PACK, S], F32)
-            for i in range(PACK):
-                first = PACK - 1 - i
-                nc.vector.tensor_copy(out=windows[:, i, :], in_=falloff[:, first : first + S])
-            decay = keep.tile([P, S, PACK], F32)
-            nc.vector.tensor_copy(out=decay[:], in_=windows[:].rearrange("p i m -> p m i"))
-            first_silu = keep.tile([P, 1], F32)
-            nc.scalar.activation(out=first_silu[:], in_=falloff[:, 0:1], func=ACT.Silu)
-            return decay
-
-        def project_values(x_codes, x_scales, v_codes, v_scales, blocks):
-            waiting = []
-            for n in blocks:
-                cols = slice(n * P, (n + 1) * P)
-                bank = psum.tile([P, TILES, P], F32, tag="bank")
-                for i in range(TILES):
-                    for c in range(PASSES):
-                        nc.tensor.matmul_mx(
-                            out=bank[:, i, :],
-                            lhsT=x_codes[:, i, c, :].bitcast(FP8X4),
-                            lhsT_scale=x_scales[:, i, c, :],
-                            rhs=w_words[:, c, cols].bitcast(FP8X4),
-                            rhs_scale=w_scales[:, c, cols],
-                            start=(c == 0),
-                            stop=(c == PASSES - 1),
-                        )
-                v_grouped = stage.tile([P, P, PACK], BF16, align_bytes=64)
-                empty_bank(n % 4 == 1, v_grouped[:], bank[:].rearrange("p i j -> p j i"))
-                waiting.append(
-                    (v_grouped[:].rearrange("p j i -> p (j i)"), v_codes[:, cols], v_scales[:, cols])
-                )
-                if len(waiting) > 1:
-                    quantise(*waiting[-2])
-            quantise(*waiting[-1])
-
-        def gate_scores(q_codes, q_scales, k_codes, k_scales, decay, name):
-            g_codes, g_scales = mx_operand(name, [P, S])
-            waiting = []
-            for mc in range(TILES):
-                cols = slice(mc * P, (mc + 1) * P)
-                bank = psum.tile([P, TILES, P], F32, tag="bank")
-                for i in range(TILES):
-                    for c in range(PASSES):
-                        nc.tensor.matmul_mx(
-                            out=bank[:, i, :],
-                            lhsT=k_codes[:, i, c, :].bitcast(FP8X4),
-                            lhsT_scale=k_scales[:, i, c, :],
-                            rhs=q_codes[:, mc, c, :].bitcast(FP8X4),
-                            rhs_scale=q_scales[:, mc, c, :],
-                            start=(c == 0),
-                            stop=(c == PASSES - 1),
-                        )
-                decayed = stage.tile([P, P, PACK], F32)
-                nc.vector.tensor_tensor(
-                    out=decayed[:],
-                    in0=bank[:].rearrange("p i m -> p m i"),
-                    in1=decay[:, cols, :],
-                    op=ALU.mult,
-                )
-                g_grouped = stage.tile([P, P, PACK], BF16, align_bytes=64)
-                nc.scalar.activation(out=g_grouped[:], in_=decayed[:], func=ACT.Silu)
-                waiting.append(
-                    (g_grouped[:].rearrange("p m i -> p (m i)"), g_codes[:, cols], g_scales[:, cols])
-                )
-                if mc > 0:
-                    quantise(*waiting[mc - 1])
-            quantise(*waiting[TILES - 1])
-            return g_codes, g_scales
-
-        def write_outputs(b, g_codes, g_scales, v_codes, v_scales):
-            for mc in range(TILES):
-                rows = slice(mc * P, (mc + 1) * P)
-                for half in range(HALVES):
-                    cols = slice(half * BANK, (half + 1) * BANK)
-                    bank = psum.tile([P, BANK], F32, tag="bank")
                     nc.tensor.matmul_mx(
-                        out=bank[:],
-                        lhsT=g_codes[:, rows].bitcast(FP8X4),
-                        lhsT_scale=g_scales[:, rows],
-                        rhs=v_codes[:, cols].bitcast(FP8X4),
-                        rhs_scale=v_scales[:, cols],
-                        start=True,
-                        stop=True,
+                        out=bank[:, i, :],
+                        lhsT=x_codes[:, i, c, :].bitcast(FP8X4),
+                        lhsT_scale=x_scales[:, i, c, :],
+                        rhs=w_words[:, c, cols].bitcast(FP8X4),
+                        rhs_scale=w_scales[:, c, cols],
+                        start=(c == 0),
+                        stop=(c == PASSES - 1),
                     )
-                    piece = results.tile([P, BANK], F32)
-                    empty_bank(half % 2 == 1, piece[:], bank[:])
-                    nc.sync.dma_start(out=out[b, rows, cols], in_=piece[:])
+            v_grouped = stage.tile([P, P, PACK], BF16, align_bytes=64)
+            empty_bank(n % 4 == 1, v_grouped[:], bank[:].rearrange("p i j -> p j i"))
+            hold_back(v_grouped[:].rearrange("p j i -> p (j i)"), v_codes[:, cols], v_scales[:, cols])
 
-        x_mx = quantise_features(x_raw[0], True, "x0")
-        decay = build_decay()
-        for b in range(B):
-            v_mx = mx_operand("v%d" % b, [P, H])
-            project_values(*x_mx, *v_mx, range(0, 4))
-            k_mx = quantise_features(k_raw[b], False, "k%d" % b)
-            project_values(*x_mx, *v_mx, range(4, 6))
-            q_mx = quantise_features(q_raw[b], False, "q%d" % b)
-            project_values(*x_mx, *v_mx, range(6, 8))
-            g_mx = gate_scores(*q_mx, *k_mx, decay, "g%d" % b)
-            if b + 1 < B:
-                x_mx = quantise_features(x_raw[b + 1], True, "x%d" % (b + 1))
-            write_outputs(b, *g_mx, *v_mx)
+        def gate_tile(q_mx, k_mx, g_mx, mc):
+            q_codes, q_scales = q_mx
+            k_codes, k_scales = k_mx
+            g_codes, g_scales = g_mx
+            cols = slice(mc * P, (mc + 1) * P)
+            bank = psum.tile([P, TILES, P], F32, tag="bank")
+            for i in range(TILES):
+                for c in range(PASSES):
+                    nc.tensor.matmul_mx(
+                        out=bank[:, i, :],
+                        lhsT=k_codes[:, i, c, :].bitcast(FP8X4),
+                        lhsT_scale=k_scales[:, i, c, :],
+                        rhs=q_codes[:, mc, c, :].bitcast(FP8X4),
+                        rhs_scale=q_scales[:, mc, c, :],
+                        start=(c == 0),
+                        stop=(c == PASSES - 1),
+                    )
+            decayed = stage.tile([P, P, PACK], F32)
+            nc.vector.tensor_tensor(
+                out=decayed[:],
+                in0=bank[:].rearrange("p i m -> p m i"),
+                in1=decay[:, cols, :],
+                op=ALU.mult,
+            )
+            g_grouped = stage.tile([P, P, PACK], BF16, align_bytes=64)
+            nc.scalar.activation(out=g_grouped[:], in_=decayed[:], func=ACT.Silu)
+            hold_back(g_grouped[:].rearrange("p m i -> p (m i)"), g_codes[:, cols], g_scales[:, cols])
+
+        def write_tile(b, g_mx, v_mx, mc):
+            g_codes, g_scales = g_mx
+            v_codes, v_scales = v_mx
+            rows = slice(mc * P, (mc + 1) * P)
+            for half in range(HALVES):
+                cols = slice(half * BANK, (half + 1) * BANK)
+                bank = psum.tile([P, BANK], F32, tag="bank")
+                nc.tensor.matmul_mx(
+                    out=bank[:],
+                    lhsT=g_codes[:, rows].bitcast(FP8X4),
+                    lhsT_scale=g_scales[:, rows],
+                    rhs=v_codes[:, cols].bitcast(FP8X4),
+                    rhs_scale=v_scales[:, cols],
+                    start=True,
+                    stop=True,
+                )
+                piece = results.tile([P, BANK], F32)
+                empty_bank(half % 2 == 1, piece[:], bank[:])
+                nc.sync.dma_start(out=out[b, rows, cols], in_=piece[:])
+
+        x_mx = [mx_operand("x%d" % b, [P, TILES, PASSES, P]) for b in range(B)]
+        k_mx = [mx_operand("k%d" % b, [P, TILES, PASSES, P]) for b in range(B)]
+        q_mx = [mx_operand("q%d" % b, [P, TILES, PASSES, P]) for b in range(B)]
+        v_mx = [mx_operand("v%d" % b, [P, H]) for b in range(B)]
+        g_mx = [mx_operand("g%d" % b, [P, S]) for b in range(B)]
+
+        def transpose_x(b):
+            for i in range(TILES):
+                transpose_tile(x_raw[b], True, x_mx[b], i)
+
+        def transpose_k(b):
+            for i in range(TILES):
+                transpose_tile(k_raw[b], False, k_mx[b], i)
+
+        def transpose_q(b):
+            for i in range(TILES):
+                transpose_tile(q_raw[b], False, q_mx[b], i)
+
+        def project(b, n):
+            project_block(x_mx[b], v_mx[b], n)
+
+        def gate(b, mc):
+            gate_tile(q_mx[b], k_mx[b], g_mx[b], mc)
+
+        def write(b, mc):
+            write_tile(b, g_mx[b], v_mx[b], mc)
+
+        windows = keep.tile([P, PACK, S], F32)
+        for i in range(PACK):
+            first = PACK - 1 - i
+            nc.vector.tensor_copy(out=windows[:, i, :], in_=falloff[:, first : first + S])
+        decay = keep.tile([P, S, PACK], F32)
+
+        transpose_x(0)
+        issue_held_back()
+        first_silu = keep.tile([P, 1], F32)
+        nc.scalar.activation(out=first_silu[:], in_=falloff[:, 0:1], func=ACT.Silu)
+        for n in range(4):
+            project(0, n)
+            cols = slice(n * P, (n + 1) * P)
+            nc.vector.tensor_copy(
+                out=decay[:, cols, :], in_=windows[:, :, cols].rearrange("p i m -> p m i")
+            )
+        transpose_k(0)
+        project(0, 4)
+        project(0, 5)
+        transpose_q(0)
+        project(0, 6)
+        project(0, 7)
+        gate(0, 0)
+        gate(0, 1)
+        transpose_x(1)
+        gate(0, 2)
+        write(0, 0)
+        gate(0, 3)
+        write(0, 1)
+        project(1, 0)
+        write(0, 2)
+        project(1, 1)
+        write(0, 3)
+        project(1, 2)
+        project(1, 3)
+        transpose_k(1)
+        project(1, 4)
+        transpose_q(1)
+        project(1, 5)
+        gate(1, 0)
+        project(1, 6)
+        gate(1, 1)
+        project(1, 7)
+        gate(1, 2)
+        write(1, 0)
+        gate(1, 3)
+        write(1, 1)
+        issue_held_back()
+        write(1, 2)
+        write(1, 3)

@@ -89,14 +89,19 @@ def tile_simpleretention_pa_kernel(tc, q, k, x, w_v_words, w_v_scales, out):
 
         held_back = []
 
-        def issue_held_back():
-            for grouped, codes, scales in held_back:
-                nc.vector.quantize_mx(out=codes.bitcast(FP8X4), scales=scales, in_=grouped)
+        def issue_held_back(units=TILES):
+            waiting = []
+            for left, grouped, codes, scales in held_back:
+                if left <= units:
+                    nc.vector.quantize_mx(out=codes.bitcast(FP8X4), scales=scales, in_=grouped)
+                else:
+                    waiting.append((left - units, grouped, codes, scales))
             held_back.clear()
+            held_back.extend(waiting)
 
-        def hold_back(grouped, codes, scales):
-            issue_held_back()
-            held_back.append((grouped, codes, scales))
+        def hold_back(units, grouped, codes, scales):
+            issue_held_back(1)
+            held_back.append((units, grouped, codes, scales))
 
         def mx_operand(name, shape):
             codes = keep.tile(shape, U32, name=name + "_codes", align_bytes=64)
@@ -125,6 +130,7 @@ def tile_simpleretention_pa_kernel(tc, q, k, x, w_v_words, w_v_scales, out):
                 i % 4 == 1, grouped[:].bitcast(F32), bank[:].rearrange("p c u r -> p c r u")
             )
             hold_back(
+                1,
                 grouped[:].rearrange("p c r t -> p (c r t)"),
                 codes[:, i].rearrange("p c r -> p (c r)"),
                 scales[:, i].rearrange("p c r -> p (c r)"),
@@ -148,7 +154,7 @@ def tile_simpleretention_pa_kernel(tc, q, k, x, w_v_words, w_v_scales, out):
                     )
             v_grouped = stage.tile([P, P, PACK], BF16, align_bytes=64)
             empty_bank(n % 4 == 1, v_grouped[:], bank[:].rearrange("p i j -> p j i"))
-            hold_back(v_grouped[:].rearrange("p j i -> p (j i)"), v_codes[:, cols], v_scales[:, cols])
+            hold_back(1, v_grouped[:].rearrange("p j i -> p (j i)"), v_codes[:, cols], v_scales[:, cols])
 
         def gate_tile(q_mx, k_mx, g_mx, mc):
             q_codes, q_scales = q_mx
@@ -176,17 +182,17 @@ def tile_simpleretention_pa_kernel(tc, q, k, x, w_v_words, w_v_scales, out):
             )
             g_grouped = stage.tile([P, P, PACK], BF16, align_bytes=64)
             nc.scalar.activation(out=g_grouped[:], in_=decayed[:], func=ACT.Silu)
-            hold_back(g_grouped[:].rearrange("p m i -> p (m i)"), g_codes[:, cols], g_scales[:, cols])
+            hold_back(2, g_grouped[:].rearrange("p m i -> p (m i)"), g_codes[:, cols], g_scales[:, cols])
 
-        def write_tile(b, g_mx, v_mx, mc):
-            g_codes, g_scales = g_mx
-            v_codes, v_scales = v_mx
-            rows = slice(mc * P, (mc + 1) * P)
-            for half in range(HALVES):
-                cols = slice(half * BANK, (half + 1) * BANK)
-                bank = psum.tile([P, BANK], F32, tag="bank")
+        def write_columns(b, on_vector, row_tiles, cols):
+            g_codes, g_scales = g_mx[b]
+            v_codes, v_scales = v_mx[b]
+            width = cols.stop - cols.start
+            bank = psum.tile([P, len(row_tiles), width], F32, tag="bank")
+            for slot, mc in enumerate(row_tiles):
+                rows = slice(mc * P, (mc + 1) * P)
                 nc.tensor.matmul_mx(
-                    out=bank[:],
+                    out=bank[:, slot, :],
                     lhsT=g_codes[:, rows].bitcast(FP8X4),
                     lhsT_scale=g_scales[:, rows],
                     rhs=v_codes[:, cols].bitcast(FP8X4),
@@ -194,9 +200,13 @@ def tile_simpleretention_pa_kernel(tc, q, k, x, w_v_words, w_v_scales, out):
                     start=True,
                     stop=True,
                 )
-                piece = results.tile([P, BANK], F32)
-                empty_bank(half % 2 == 1, piece[:], bank[:])
-                nc.sync.dma_start(out=out[b, rows, cols], in_=piece[:])
+            piece = results.tile([P, len(row_tiles), width], F32)
+            empty_bank(on_vector, piece[:], bank[:])
+            issue_held_back(1)
+            rows = slice(row_tiles[0] * P, (row_tiles[-1] + 1) * P)
+            nc.sync.dma_start(
+                out=out[b, rows, cols].rearrange("(m p) h -> p m h", p=P), in_=piece[:]
+            )
 
         x_mx = [mx_operand("x%d" % b, [P, TILES, PASSES, P]) for b in range(B)]
         k_mx = [mx_operand("k%d" % b, [P, TILES, PASSES, P]) for b in range(B)]
@@ -222,8 +232,9 @@ def tile_simpleretention_pa_kernel(tc, q, k, x, w_v_words, w_v_scales, out):
         def gate(b, mc):
             gate_tile(q_mx[b], k_mx[b], g_mx[b], mc)
 
-        def write(b, mc):
-            write_tile(b, g_mx[b], v_mx[b], mc)
+        def write_row(b, mc):
+            for half in range(HALVES):
+                write_columns(b, half == 1, [mc], slice(half * BANK, (half + 1) * BANK))
 
         windows = keep.tile([P, PACK, S], F32)
         for i in range(PACK):
@@ -247,31 +258,29 @@ def tile_simpleretention_pa_kernel(tc, q, k, x, w_v_words, w_v_scales, out):
         transpose_q(0)
         project(0, 6)
         project(0, 7)
-        gate(0, 0)
-        gate(0, 1)
+        for mc in range(TILES):
+            gate(0, mc)
         transpose_x(1)
-        gate(0, 2)
-        write(0, 0)
-        gate(0, 3)
-        write(0, 1)
+        write_row(0, 0)
+        write_row(0, 1)
+        transpose_k(1)
         project(1, 0)
-        write(0, 2)
         project(1, 1)
-        write(0, 3)
+        write_row(0, 2)
+        transpose_q(1)
+        write_row(0, 3)
         project(1, 2)
         project(1, 3)
-        transpose_k(1)
+        for mc in range(TILES):
+            gate(1, mc)
         project(1, 4)
-        transpose_q(1)
         project(1, 5)
-        gate(1, 0)
+        for mc in range(TILES):
+            write_columns(1, mc % 2 == 1, [mc], slice(0, BANK))
         project(1, 6)
-        gate(1, 1)
         project(1, 7)
-        gate(1, 2)
-        write(1, 0)
-        gate(1, 3)
-        write(1, 1)
+        for pair in range(2):
+            write_columns(1, pair == 1, [2 * pair, 2 * pair + 1], slice(BANK, BANK + 2 * P))
         issue_held_back()
-        write(1, 2)
-        write(1, 3)
+        for pair in range(2):
+            write_columns(1, pair == 1, [2 * pair, 2 * pair + 1], slice(BANK + 2 * P, H))

@@ -25,6 +25,7 @@ TILES = S // P
 WORDS = K_PASS // 2
 BANK = 512
 BANKS = 8
+WARM_UP = 5
 HALVES = H // BANK
 KEYS = "(p i) h -> i p h"
 QUERIES = "(i p) h -> i p h"
@@ -41,6 +42,11 @@ def tile_simpleretention_pa_kernel(tc, q, k, x, w_v_words, w_v_scales, out):
         psum = ctx.enter_context(tc.psum_pool(name="psum", bufs=BANKS))
         ctx.enter_context(tc.manual_schedule())
 
+        ones = keep.tile([P, BANK], BF16)
+        nc.vector.memset(ones[:], 1.0)
+        warm_up = psum.tile([P, BANK], F32, tag="bank")
+        for i in range(WARM_UP):
+            nc.tensor.matmul(warm_up[:], lhsT=ones[:, :P], rhs=ones[:], start=True, stop=True)
         w_scales = keep.tile([P, PASSES, H], U8, align_bytes=64)
         nc.vector.memset(w_scales[:].bitcast(I32), 0)
         ident = keep.tile([P, P], F32)

@@ -25,7 +25,6 @@ TILES = S // P
 WORDS = K_PASS // 2
 BANK = 512
 BANKS = 8
-WARM_UP = 5
 HALVES = H // BANK
 KEYS = "(p i) h -> i p h"
 QUERIES = "(i p) h -> i p h"
@@ -42,11 +41,21 @@ def tile_simpleretention_pa_kernel(tc, q, k, x, w_v_words, w_v_scales, out):
         psum = ctx.enter_context(tc.psum_pool(name="psum", bufs=BANKS))
         ctx.enter_context(tc.manual_schedule())
 
-        ones = keep.tile([P, BANK], BF16)
+        ones = keep.tile([P, P], BF16)
         nc.vector.memset(ones[:], 1.0)
-        warm_up = psum.tile([P, BANK], F32, tag="bank")
-        for i in range(WARM_UP):
-            nc.tensor.matmul(warm_up[:], lhsT=ones[:, :P], rhs=ones[:], start=True, stop=True)
+
+        def keep_warm(count):
+            unread = psum.tile([P, BANK], F32, tag="bank")
+            for i in range(count):
+                nc.tensor.matmul(
+                    unread[:],
+                    lhsT=ones[:],
+                    rhs=ones[:, 0:1].to_broadcast([P, BANK]),
+                    start=True,
+                    stop=True,
+                )
+
+        keep_warm(4)
         w_scales = keep.tile([P, PASSES, H], U8, align_bytes=64)
         nc.vector.memset(w_scales[:].bitcast(I32), 0)
         ident = keep.tile([P, P], F32)
@@ -220,10 +229,6 @@ def tile_simpleretention_pa_kernel(tc, q, k, x, w_v_words, w_v_scales, out):
         v_mx = [mx_operand("v%d" % b, [P, H]) for b in range(B)]
         g_mx = [mx_operand("g%d" % b, [P, S]) for b in range(B)]
 
-        def transpose_x(b):
-            for i in range(TILES):
-                transpose_tile(x_raw[b], True, x_mx[b], i)
-
         def transpose_k(b):
             for i in range(TILES):
                 transpose_tile(k_raw[b], False, k_mx[b], i)
@@ -248,7 +253,11 @@ def tile_simpleretention_pa_kernel(tc, q, k, x, w_v_words, w_v_scales, out):
             nc.vector.tensor_copy(out=windows[:, i, :], in_=falloff[:, first : first + S])
         decay = keep.tile([P, S, PACK], F32)
 
-        transpose_x(0)
+        for i in range(TILES):
+            transpose_tile(x_raw[0], True, x_mx[0], i)
+            if i == 1 or i == 2:
+                keep_warm(1)
+        keep_warm(2)
         issue_held_back()
         first_silu = keep.tile([P, 1], F32)
         nc.scalar.activation(out=first_silu[:], in_=falloff[:, 0:1], func=ACT.Silu)
@@ -266,7 +275,8 @@ def tile_simpleretention_pa_kernel(tc, q, k, x, w_v_words, w_v_scales, out):
         project(0, 7)
         for mc in range(TILES):
             gate(0, mc)
-        transpose_x(1)
+        for i in range(TILES):
+            transpose_tile(x_raw[1], True, x_mx[1], i)
         write_row(0, 0)
         write_row(0, 1)
         transpose_k(1)

@@ -56,7 +56,7 @@ def tile_simpleretention_pa_kernel(tc, q, k, x, w_v_words, w_v_scales, out):
                 )
 
         keep_warm(4)
-        w_scales = keep.tile([P, PASSES, H], U8, align_bytes=64)
+        w_scales = keep.tile([P, H], U8, align_bytes=64)
         nc.vector.memset(w_scales[:].bitcast(I32), 0)
         ident = keep.tile([P, P], F32)
         make_identity(nc, ident[:])
@@ -72,35 +72,36 @@ def tile_simpleretention_pa_kernel(tc, q, k, x, w_v_words, w_v_scales, out):
         nc.scalar.activation(out=falloff[:], in_=offset[:], func=ACT.Abs)
         nc.scalar.activation(out=falloff[:], in_=falloff[:], func=ACT.Exp, scale=math.log(GAMMA))
 
-        def load_tokens(rows, view, name):
-            raw = keep.tile([P, TILES, H], BF16, name=name)
-            tiles = rows.rearrange(view, p=P)
-            for i in range(TILES):
-                nc.sync.dma_start(out=raw[:, i, :], in_=tiles[i])
-            return raw
+        def token_tiles(name):
+            return keep.tile([P, TILES, H], BF16, name=name)
 
-        x_raw = [load_tokens(x[0], KEYS, "x_raw0")]
-        k_raw = []
-        q_raw = []
+        def load_tokens(raw, rows, view, tiles):
+            for i in tiles:
+                nc.sync.dma_start(out=raw[:, i, :], in_=rows.rearrange(view, p=P)[i])
+
+        x_raw = [token_tiles("x_raw%d" % b) for b in range(B)]
+        k_raw = [token_tiles("k_raw%d" % b) for b in range(B)]
+        q_raw = [token_tiles("q_raw%d" % b) for b in range(B)]
+        load_tokens(x_raw[0], x[0], KEYS, range(TILES))
+        load_tokens(k_raw[0], k[0], KEYS, range(0, 2))
         for quadrant in range(4):
+            first = 32 * quadrant
             nc.sync.dma_start(
-                out=w_scales[32 * quadrant : 32 * quadrant + 4].bitcast(I32),
-                in_=w_v_scales[:, 4 * quadrant : 4 * quadrant + 4, :]
-                .rearrange("c r j -> r c j")
-                .bitcast(I32),
+                out=w_scales[first : first + 4 * PASSES].bitcast(I32),
+                in_=w_v_scales[:, 4 * quadrant : 4 * quadrant + 4, :].bitcast(I32),
             )
         w_words = keep.tile([P, PASSES, H], U32, align_bytes=64)
         w_bytes = w_v_words.rearrange("c p j t -> p c (j t)")
-        for half in range(HALVES):
+        for first, end in ((0, 2 * P), (2 * P, BANK), (BANK, H)):
             nc.sync.dma_start(
-                out=w_words[:, :, half * BANK : (half + 1) * BANK].bitcast(I32),
-                in_=w_bytes[:, :, half * BANK * PACK : (half + 1) * BANK * PACK].bitcast(I32),
+                out=w_words[:, :, first:end].bitcast(I32),
+                in_=w_bytes[:, :, first * PACK : end * PACK].bitcast(I32),
             )
-        for b in range(B):
-            k_raw.append(load_tokens(k[b], KEYS, "k_raw%d" % b))
-            q_raw.append(load_tokens(q[b], QUERIES, "q_raw%d" % b))
-            if b + 1 < B:
-                x_raw.append(load_tokens(x[b + 1], KEYS, "x_raw%d" % (b + 1)))
+        load_tokens(k_raw[0], k[0], KEYS, range(2, TILES))
+        load_tokens(q_raw[0], q[0], QUERIES, range(TILES))
+        load_tokens(x_raw[1], x[1], KEYS, range(TILES))
+        load_tokens(k_raw[1], k[1], KEYS, range(TILES))
+        load_tokens(q_raw[1], q[1], QUERIES, range(TILES))
 
         held_back = []
 
@@ -130,25 +131,29 @@ def tile_simpleretention_pa_kernel(tc, q, k, x, w_v_words, w_v_scales, out):
                 nc.scalar.copy(out=out_view, in_=bank_view)
 
         def transpose_tile(raw, every_second_word, operand, i):
+            transpose_passes(raw, every_second_word, operand, i, range(PASSES), i % 4 == 1)
+
+        def transpose_passes(raw, every_second_word, operand, i, passes, on_vector):
             codes, scales = operand
             words = raw[:].bitcast(F32)
-            bank = psum.tile([P, PASSES, 2, P], F32, tag="bank")
-            for c in range(PASSES):
+            bank = psum.tile([P, len(passes), 2, P], F32, tag="bank")
+            for slot, c in enumerate(passes):
                 for u in range(2):
                     if every_second_word:
                         cols = slice(WORDS * c + u, WORDS * (c + 1), 2)
                     else:
                         cols = slice(WORDS * c + P * u, WORDS * c + P * (u + 1))
-                    nc.tensor.transpose(bank[:, c, u, :], words[:, i, cols], ident[:])
-            grouped = stage.tile([P, PASSES, P, PACK], BF16, align_bytes=64)
+                    nc.tensor.transpose(bank[:, slot, u, :], words[:, i, cols], ident[:])
+            grouped = stage.tile([P, len(passes), P, PACK], BF16, align_bytes=64)
             empty_bank(
-                i % 4 == 1, grouped[:].bitcast(F32), bank[:].rearrange("p c u r -> p c r u")
+                on_vector, grouped[:].bitcast(F32), bank[:].rearrange("p c u r -> p c r u")
             )
+            span = slice(passes[0], passes[-1] + 1)
             hold_back(
                 1,
                 grouped[:].rearrange("p c r t -> p (c r t)"),
-                codes[:, i].rearrange("p c r -> p (c r)"),
-                scales[:, i].rearrange("p c r -> p (c r)"),
+                codes[:, i, span].rearrange("p c r -> p (c r)"),
+                scales[:, i, span].rearrange("p c r -> p (c r)"),
             )
 
         def project_block(x_mx, v_mx, n):
@@ -163,7 +168,7 @@ def tile_simpleretention_pa_kernel(tc, q, k, x, w_v_words, w_v_scales, out):
                         lhsT=x_codes[:, i, c, :].bitcast(FP8X4),
                         lhsT_scale=x_scales[:, i, c, :],
                         rhs=w_words[:, c, cols].bitcast(FP8X4),
-                        rhs_scale=w_scales[:, c, cols],
+                        rhs_scale=w_scales[4 * c :, cols],
                         start=(c == 0),
                         stop=(c == PASSES - 1),
                     )
@@ -229,13 +234,9 @@ def tile_simpleretention_pa_kernel(tc, q, k, x, w_v_words, w_v_scales, out):
         v_mx = [mx_operand("v%d" % b, [P, H]) for b in range(B)]
         g_mx = [mx_operand("g%d" % b, [P, S]) for b in range(B)]
 
-        def transpose_k(b):
+        def transpose_all(raw, every_second_word, operand):
             for i in range(TILES):
-                transpose_tile(k_raw[b], False, k_mx[b], i)
-
-        def transpose_q(b):
-            for i in range(TILES):
-                transpose_tile(q_raw[b], False, q_mx[b], i)
+                transpose_tile(raw, every_second_word, operand, i)
 
         def project(b, n):
             project_block(x_mx[b], v_mx[b], n)
@@ -253,11 +254,14 @@ def tile_simpleretention_pa_kernel(tc, q, k, x, w_v_words, w_v_scales, out):
             nc.vector.tensor_copy(out=windows[:, i, :], in_=falloff[:, first : first + S])
         decay = keep.tile([P, S, PACK], F32)
 
-        for i in range(TILES):
+        for i in range(TILES - 1):
             transpose_tile(x_raw[0], True, x_mx[0], i)
             if i == 1 or i == 2:
                 keep_warm(1)
-        keep_warm(2)
+        for c in range(PASSES):
+            transpose_passes(x_raw[0], True, x_mx[0], TILES - 1, range(c, c + 1), c == 1)
+        for i in range(2):
+            transpose_tile(k_raw[0], False, k_mx[0], i)
         issue_held_back()
         first_silu = keep.tile([P, 1], F32)
         nc.scalar.activation(out=first_silu[:], in_=falloff[:, 0:1], func=ACT.Silu)
@@ -267,23 +271,23 @@ def tile_simpleretention_pa_kernel(tc, q, k, x, w_v_words, w_v_scales, out):
             nc.vector.tensor_copy(
                 out=decay[:, cols, :], in_=windows[:, :, cols].rearrange("p i m -> p m i")
             )
-        transpose_k(0)
+        for i in range(2, TILES):
+            transpose_tile(k_raw[0], False, k_mx[0], i)
         project(0, 4)
         project(0, 5)
-        transpose_q(0)
+        transpose_all(q_raw[0], False, q_mx[0])
         project(0, 6)
         project(0, 7)
         for mc in range(TILES):
             gate(0, mc)
-        for i in range(TILES):
-            transpose_tile(x_raw[1], True, x_mx[1], i)
+        transpose_all(x_raw[1], True, x_mx[1])
         write_row(0, 0)
         write_row(0, 1)
-        transpose_k(1)
+        transpose_all(k_raw[1], False, k_mx[1])
         project(1, 0)
         project(1, 1)
         write_row(0, 2)
-        transpose_q(1)
+        transpose_all(q_raw[1], False, q_mx[1])
         write_row(0, 3)
         project(1, 2)
         project(1, 3)
@@ -292,9 +296,9 @@ def tile_simpleretention_pa_kernel(tc, q, k, x, w_v_words, w_v_scales, out):
         project(1, 4)
         project(1, 5)
         for mc in range(TILES):
+            if mc >= 2:
+                project(1, 4 + mc)
             write_columns(1, mc % 2 == 1, [mc], slice(0, BANK))
-        project(1, 6)
-        project(1, 7)
         for pair in range(2):
             write_columns(1, pair == 1, [2 * pair, 2 * pair + 1], slice(BANK, BANK + 2 * P))
         issue_held_back()

import math
from contextlib import ExitStack

import concourse.mybir as mybir
from concourse.masks import make_identity

F32 = mybir.dt.float32
BF16 = mybir.dt.bfloat16
I32 = mybir.dt.int32
U32 = mybir.dt.uint32
U8 = mybir.dt.uint8
FP8X4 = mybir.dt.float8_e4m3fn_x4
ACT = mybir.ActivationFunctionType
ALU = mybir.AluOpType

B = 2
S = 512
H = 1024
GAMMA = 0.96875
P = 128
PACK = 4
K_PASS = P * PACK
PASSES = H // K_PASS
TILES = S // P
WORDS = K_PASS // 2
BANK = 512
BANKS = 8
HALVES = H // BANK
KEYS = "(p i) h -> i p h"
QUERIES = "(i p) h -> i p h"

FLOPS = 2 * B * (S * H * H + 2 * S * S * H)


def tile_simpleretention_pa_kernel(tc, q, k, x, w_v_words, w_v_scales, out):
    nc = tc.nc
    with ExitStack() as ctx:
        keep = ctx.enter_context(tc.tile_pool(name="keep", bufs=1))
        stage = ctx.enter_context(tc.tile_pool(name="stage", bufs=6))
        results = ctx.enter_context(tc.tile_pool(name="results", bufs=S * H // (P * BANK)))
        psum = ctx.enter_context(tc.psum_pool(name="psum", bufs=BANKS))
        ctx.enter_context(tc.manual_schedule())

        ones = keep.tile([P, P], BF16)
        nc.vector.memset(ones[:], 1.0)

        def keep_warm(count):
            unread = psum.tile([P, BANK], F32, tag="bank")
            for i in range(count):
                nc.tensor.matmul(
                    unread[:],
                    lhsT=ones[:],
                    rhs=ones[:, 0:1].to_broadcast([P, BANK]),
                    start=True,
                    stop=True,
                )

        keep_warm(4)
        w_scales = keep.tile([P, H], U8, align_bytes=64)
        nc.vector.memset(w_scales[:].bitcast(I32), 0)
        ident = keep.tile([P, P], F32)
        make_identity(nc, ident[:])
        offset = keep.tile([P, S + PACK - 1], F32)
        nc.gpsimd.iota(
            offset[:],
            pattern=[[1, S + PACK - 1]],
            base=-(PACK - 1),
            channel_multiplier=-PACK,
            allow_small_or_imprecise_dtypes=True,
        )
        falloff = keep.tile([P, S + PACK - 1], F32)
        nc.scalar.activation(out=falloff[:], in_=offset[:], func=ACT.Abs)
        nc.scalar.activation(out=falloff[:], in_=falloff[:], func=ACT.Exp, scale=math.log(GAMMA))

        def token_tiles(name):
            return keep.tile([P, TILES, H], BF16, name=name)

        def load_tokens(raw, rows, view, tiles):
            for i in tiles:
                nc.sync.dma_start(out=raw[:, i, :], in_=rows.rearrange(view, p=P)[i])

        x_raw = [token_tiles("x_raw%d" % b) for b in range(B)]
        k_raw = [token_tiles("k_raw%d" % b) for b in range(B)]
        q_raw = [token_tiles("q_raw%d" % b) for b in range(B)]
        load_tokens(x_raw[0], x[0], KEYS, range(TILES))
        load_tokens(k_raw[0], k[0], KEYS, range(0, 2))
        for quadrant in range(4):
            first = 32 * quadrant
            nc.sync.dma_start(
                out=w_scales[first : first + 4 * PASSES].bitcast(I32),
                in_=w_v_scales[:, 4 * quadrant : 4 * quadrant + 4, :].bitcast(I32),
            )
        w_words = keep.tile([P, PASSES, H], U32, align_bytes=64)
        w_bytes = w_v_words.rearrange("c p j t -> p c (j t)")
        for first, end in ((0, 2 * P), (2 * P, BANK), (BANK, H)):
            nc.sync.dma_start(
                out=w_words[:, :, first:end].bitcast(I32),
                in_=w_bytes[:, :, first * PACK : end * PACK].bitcast(I32),
            )
        load_tokens(k_raw[0], k[0], KEYS, range(2, TILES))
        load_tokens(q_raw[0], q[0], QUERIES, range(TILES))
        load_tokens(x_raw[1], x[1], KEYS, range(TILES))
        load_tokens(k_raw[1], k[1], KEYS, range(TILES))
        load_tokens(q_raw[1], q[1], QUERIES, range(TILES))

        held_back = []

        def issue_held_back(units=TILES):
            waiting = []
            for left, grouped, codes, scales in held_back:
                if left <= units:
                    nc.vector.quantize_mx(out=codes.bitcast(FP8X4), scales=scales, in_=grouped)
                else:
                    waiting.append((left - units, grouped, codes, scales))
            held_back.clear()
            held_back.extend(waiting)

        def hold_back(units, grouped, codes, scales):
            issue_held_back(1)
            held_back.append((units, grouped, codes, scales))

        def mx_operand(name, shape):
            codes = keep.tile(shape, U32, name=name + "_codes", align_bytes=64)
            scales = keep.tile(shape, U8, name=name + "_scales", align_bytes=64)
            return codes, scales

        def empty_bank(on_vector, out_view, bank_view):
            if on_vector:
                nc.vector.tensor_copy(out=out_view, in_=bank_view)
            else:
                nc.scalar.copy(out=out_view, in_=bank_view)

        def transpose_tile(raw, every_second_word, operand, i):
            transpose_passes(raw, every_second_word, operand, i, range(PASSES), i % 4 == 1)

        def transpose_passes(raw, every_second_word, operand, i, passes, on_vector):
            codes, scales = operand
            words = raw[:].bitcast(F32)
            bank = psum.tile([P, len(passes), 2, P], F32, tag="bank")
            for slot, c in enumerate(passes):
                for u in range(2):
                    if every_second_word:
                        cols = slice(WORDS * c + u, WORDS * (c + 1), 2)
                    else:
                        cols = slice(WORDS * c + P * u, WORDS * c + P * (u + 1))
                    nc.tensor.transpose(bank[:, slot, u, :], words[:, i, cols], ident[:])
            grouped = stage.tile([P, len(passes), P, PACK], BF16, align_bytes=64)
            empty_bank(
                on_vector, grouped[:].bitcast(F32), bank[:].rearrange("p c u r -> p c r u")
            )
            span = slice(passes[0], passes[-1] + 1)
            hold_back(
                1,
                grouped[:].rearrange("p c r t -> p (c r t)"),
                codes[:, i, span].rearrange("p c r -> p (c r)"),
                scales[:, i, span].rearrange("p c r -> p (c r)"),
            )

        def project_block(x_mx, v_mx, n):
            x_codes, x_scales = x_mx
            v_codes, v_scales = v_mx
            cols = slice(n * P, (n + 1) * P)
            bank = psum.tile([P, TILES, P], F32, tag="bank")
            for i in range(TILES):
                for c in range(PASSES):
                    nc.tensor.matmul_mx(
                        out=bank[:, i, :],
                        lhsT=x_codes[:, i, c, :].bitcast(FP8X4),
                        lhsT_scale=x_scales[:, i, c, :],
                        rhs=w_words[:, c, cols].bitcast(FP8X4),
                        rhs_scale=w_scales[4 * c :, cols],
                        start=(c == 0),
                        stop=(c == PASSES - 1),
                    )
            v_grouped = stage.tile([P, P, PACK], BF16, align_bytes=64)
            empty_bank(n % 4 == 1, v_grouped[:], bank[:].rearrange("p i j -> p j i"))
            hold_back(1, v_grouped[:].rearrange("p j i -> p (j i)"), v_codes[:, cols], v_scales[:, cols])

        def gate_tile(q_mx, k_mx, g_mx, mc):
            q_codes, q_scales = q_mx
            k_codes, k_scales = k_mx
            g_codes, g_scales = g_mx
            cols = slice(mc * P, (mc + 1) * P)
            bank = psum.tile([P, TILES, P], F32, tag="bank")
            for i in range(TILES):
                for c in range(PASSES):
                    nc.tensor.matmul_mx(
                        out=bank[:, i, :],
                        lhsT=k_codes[:, i, c, :].bitcast(FP8X4),
                        lhsT_scale=k_scales[:, i, c, :],
                        rhs=q_codes[:, mc, c, :].bitcast(FP8X4),
                        rhs_scale=q_scales[:, mc, c, :],
                        start=(c == 0),
                        stop=(c == PASSES - 1),
                    )
            decayed = stage.tile([P, P, PACK], F32)
            nc.vector.tensor_tensor(
                out=decayed[:],
                in0=bank[:].rearrange("p i m -> p m i"),
                in1=decay[:, cols, :],
                op=ALU.mult,
            )
            g_grouped = stage.tile([P, P, PACK], BF16, align_bytes=64)
            nc.scalar.activation(out=g_grouped[:], in_=decayed[:], func=ACT.Silu)
            hold_back(2, g_grouped[:].rearrange("p m i -> p (m i)"), g_codes[:, cols], g_scales[:, cols])

        def write_columns(b, on_vector, row_tiles, cols):
            g_codes, g_scales = g_mx[b]
            v_codes, v_scales = v_mx[b]
            width = cols.stop - cols.start
            bank = psum.tile([P, len(row_tiles), width], F32, tag="bank")
            for slot, mc in enumerate(row_tiles):
                rows = slice(mc * P, (mc + 1) * P)
                nc.tensor.matmul_mx(
                    out=bank[:, slot, :],
                    lhsT=g_codes[:, rows].bitcast(FP8X4),
                    lhsT_scale=g_scales[:, rows],
                    rhs=v_codes[:, cols].bitcast(FP8X4),
                    rhs_scale=v_scales[:, cols],
                    start=True,
                    stop=True,
                )
            piece = results.tile([P, len(row_tiles), width], F32)
            empty_bank(on_vector, piece[:], bank[:])
            issue_held_back(1)
            rows = slice(row_tiles[0] * P, (row_tiles[-1] + 1) * P)
            nc.sync.dma_start(
                out=out[b, rows, cols].rearrange("(m p) h -> p m h", p=P), in_=piece[:]
            )

        x_mx = [mx_operand("x%d" % b, [P, TILES, PASSES, P]) for b in range(B)]
        k_mx = [mx_operand("k%d" % b, [P, TILES, PASSES, P]) for b in range(B)]
        q_mx = [mx_operand("q%d" % b, [P, TILES, PASSES, P]) for b in range(B)]
        v_mx = [mx_operand("v%d" % b, [P, H]) for b in range(B)]
        g_mx = [mx_operand("g%d" % b, [P, S]) for b in range(B)]

        def transpose_all(raw, every_second_word, operand):
            for i in range(TILES):
                transpose_tile(raw, every_second_word, operand, i)

        def project(b, n):
            project_block(x_mx[b], v_mx[b], n)

        def gate(b, mc):
            gate_tile(q_mx[b], k_mx[b], g_mx[b], mc)

        def write_row(b, mc):
            for half in range(HALVES):
                write_columns(b, half == 1, [mc], slice(half * BANK, (half + 1) * BANK))

        windows = keep.tile([P, PACK, S], F32)
        for i in range(PACK):
            first = PACK - 1 - i
            nc.vector.tensor_copy(out=windows[:, i, :], in_=falloff[:, first : first + S])
        decay = keep.tile([P, S, PACK], F32)

        for i in range(TILES - 1):
            transpose_tile(x_raw[0], True, x_mx[0], i)
            if i == 1 or i == 2:
                keep_warm(1)
        for c in range(PASSES):
            transpose_passes(x_raw[0], True, x_mx[0], TILES - 1, range(c, c + 1), c == 1)
        for i in range(2):
            transpose_tile(k_raw[0], False, k_mx[0], i)
        issue_held_back()
        first_silu = keep.tile([P, 1], F32)
        nc.scalar.activation(out=first_silu[:], in_=falloff[:, 0:1], func=ACT.Silu)
        for n in range(4):
            project(0, n)
            cols = slice(n * P, (n + 1) * P)
            nc.vector.tensor_copy(
                out=decay[:, cols, :], in_=windows[:, :, cols].rearrange("p i m -> p m i")
            )
        for i in range(2, TILES):
            transpose_tile(k_raw[0], False, k_mx[0], i)
        project(0, 4)
        project(0, 5)
        transpose_all(q_raw[0], False, q_mx[0])
        project(0, 6)
        project(0, 7)
        for mc in range(TILES):
            gate(0, mc)
        transpose_all(x_raw[1], True, x_mx[1])
        write_row(0, 0)
        write_row(0, 1)
        transpose_all(k_raw[1], False, k_mx[1])
        project(1, 0)
        project(1, 1)
        write_row(0, 2)
        transpose_all(q_raw[1], False, q_mx[1])
        write_row(0, 3)
        project(1, 2)
        project(1, 3)
        for mc in range(TILES):
            gate(1, mc)
        project(1, 4)
        project(1, 5)
        for mc in range(TILES):
            if mc >= 2:
                project(1, 4 + mc)
            write_columns(1, mc % 2 == 1, [mc], slice(0, BANK))
        for pair in range(2):
            write_columns(1, pair == 1, [2 * pair, 2 * pair + 1], slice(BANK, BANK + 2 * P))
        issue_held_back()
        for pair in range(2):
            write_columns(1, pair == 1, [2 * pair, 2 * pair + 1], slice(BANK + 2 * P, H))
